import numpy as np
import ml_dtypes


def mxq(x, axis, fmt="e4m3"):
    dtype, down = {"e4m3": (ml_dtypes.float8_e4m3fn, 7), "e5m2": (ml_dtypes.float8_e5m2, 14)}[fmt]
    v = np.moveaxis(np.asarray(x, np.float32).astype(ml_dtypes.bfloat16).astype(np.float64), axis, -1)
    blocks = v.reshape(v.shape[:-1] + (-1, 32))
    amax = np.abs(blocks).max(-1, keepdims=True)
    byte = np.maximum(np.where(amax > 0, np.frexp(amax)[1] - 1 + 127, 0) - down, 1)
    scale = np.exp2(byte - 127.0)
    codes = (blocks / scale).astype(np.float32).astype(dtype).astype(np.float64)
    return np.moveaxis((codes * scale).reshape(v.shape), -1, axis)


WIDE = False


def mx_kscale(k):
    if not WIDE:
        return np.ones(k)
    levels = np.array([10, -10, 5, -5, 0])
    if k % 512:
        return np.exp2(np.random.permutation(np.resize(levels, k // 32))).repeat(32)
    a = np.empty((k // 512, 16))
    for p in range(k // 512):
        a[p, :8] = np.random.permutation(np.resize(levels, 8))
        for g in range(8):
            far = levels[np.abs(levels - a[p, g]) >= 10]
            a[p, g + 8] = far[np.random.randint(len(far))]
    return np.exp2(a.ravel()).repeat(32)


BF16 = ml_dtypes.bfloat16


def bf(x):
    return np.asarray(x, np.float32).astype(BF16)


def f64(x):
    return np.asarray(x).astype(np.float64)


B, S, H, NH, HD = 4, 2048, 1024, 2, 64
E = NH * HD
HALF = HD // 2


def rope_tables():
    inv_freq = 1.0 / 10000.0 ** (np.arange(0, HD, 2) / HD)
    pos = np.random.randint(0, S) + np.arange(S)
    freqs = np.outer(pos, inv_freq)
    emb = np.concatenate([freqs, freqs], axis=-1)
    return bf(np.cos(emb)), bf(np.sin(emb))


def apply_rotary(x, cos, sin):
    c = cos[None, None, :, :]
    s = sin[None, None, :, :]
    x1, x2 = x[..., :HALF], x[..., HALF:]
    rotated = np.concatenate([-x2, x1], axis=-1)
    return x * c + rotated * s


def setup_inputs():
    s = mx_kscale(H)
    cos, sin = rope_tables()
    return {"hidden_states": bf(np.random.standard_normal((B, S, H)) * s),
            "cos": cos, "sin": sin,
            "w_qkv": bf(np.random.standard_normal((3 * E, H)) / np.sqrt(H) / s[None, :])}


def reference(hidden_states, cos, sin, w_qkv):
    qkv = mxq(f64(hidden_states), 2, "e4m3") @ mxq(f64(w_qkv), 1, "e4m3").T
    qkv = qkv.reshape(B, S, 3, NH, HD).transpose(2, 0, 3, 1, 4)
    q, k, v = qkv[0], qkv[1], qkv[2]
    q = apply_rotary(q, f64(cos), f64(sin))
    k = apply_rotary(k, f64(cos), f64(sin))
    return q, k, v

@@ -1,0 +1,203 @@
+from contextlib import ExitStack
+
+import concourse.mybir as mybir
+from concourse.masks import make_identity
+
+BF16 = mybir.dt.bfloat16
+F32 = mybir.dt.float32
+U32 = mybir.dt.uint32
+U8 = mybir.dt.uint8
+FP8X4 = mybir.dt.float8_e4m3fn_x4
+MULT = mybir.AluOpType.mult
+ADD = mybir.AluOpType.add
+
+B, S, H, NH, HD = 4, 2048, 1024, 2, 64
+E = NH * HD
+HALF = HD // 2
+P = 128
+PACK = 4
+PASSES = H // (P * PACK)
+ROW_WORDS = H // 2
+WORD_BLOCKS = ROW_WORDS // P
+POS = S // P
+ROUND_TILES = 4
+ROUNDS_PER_BATCH = POS // ROUND_TILES
+ROUNDS = B * ROUNDS_PER_BATCH
+STORE_TILES = 8
+LOOKAHEAD = 5
+
+FLOPS = 2 * B * S * H * 3 * E
+
+
+def tile_flashattention_pa_t_kernel(tc, hidden_states, cos, sin, w_qkv, out_0, out_1, out_2):
+    nc = tc.nc
+    outs = (out_0, out_1, out_2)
+
+    with ExitStack() as ctx:
+        ctx.enter_context(tc.manual_schedule())
+        const = ctx.enter_context(tc.tile_pool(name="const", bufs=1))
+        x_pool = ctx.enter_context(tc.tile_pool(name="x", bufs=LOOKAHEAD))
+        grouped_pool = ctx.enter_context(tc.tile_pool(name="grouped", bufs=6))
+        code_pool = ctx.enter_context(tc.tile_pool(name="codes", bufs=3))
+        sin_pool = ctx.enter_context(tc.tile_pool(name="sin_part", bufs=3))
+        res_pool = ctx.enter_context(tc.tile_pool(name="res", bufs=3))
+        xt_pool = ctx.enter_context(tc.psum_pool(name="xt", bufs=4))
+        qk_pool = ctx.enter_context(tc.psum_pool(name="qk", bufs=2))
+        v_pool = ctx.enter_context(tc.psum_pool(name="v", bufs=2))
+
+        def transpose_rows(words):
+            xt = xt_pool.tile([P, WORD_BLOCKS, P], F32)
+            for blk in range(WORD_BLOCKS):
+                g, u = divmod(blk, 2)
+                nc.tensor.transpose(xt[:, blk, :], words[:, 2 * P * g + u : 2 * P * (g + 1) : 2], ident[:])
+            return xt
+
+        def regroup(dst_words, xt):
+            nc.scalar.copy(out=dst_words, in_=xt[:].rearrange("p (g u) r -> p g r u", u=2))
+
+        ident = const.tile([P, P], F32)
+        make_identity(nc, ident[:])
+
+        w_sb = const.tile([P, 3 * H], BF16)
+        nc.sync.dma_start(
+            out=w_sb[:].rearrange("p (a k) -> p a k", a=3), in_=w_qkv.rearrange("(a p) k -> p a k", p=P)
+        )
+
+        def load_round(r):
+            b, quarter = divmod(r, ROUNDS_PER_BATCH)
+            x_sb = x_pool.tile([P, ROUND_TILES * H], BF16)
+            rows = hidden_states[b].rearrange("(p j) k -> p (j k)", j=POS)
+            nc.sync.dma_start(out=x_sb[:], in_=rows[:, quarter * ROUND_TILES * H : (quarter + 1) * ROUND_TILES * H])
+            return x_sb
+
+        x_tiles = {}
+        x_tiles[0] = load_round(0)
+
+        cos_sb = const.tile([P, POS, HD], BF16)
+        sin_sb = const.tile([P, POS, HD], BF16)
+        nc.sync.dma_start(out=cos_sb[:], in_=cos.rearrange("(p j) d -> p j d", j=POS))
+        nc.sync.dma_start(out=sin_sb[:], in_=sin.rearrange("(p j) d -> p j d", j=POS))
+        nc.vector.tensor_scalar_mul(out=sin_sb[:, :, 0:HALF], in0=sin_sb[:, :, 0:HALF], scalar1=-1.0)
+
+        for r in range(1, LOOKAHEAD):
+            x_tiles[r] = load_round(r)
+
+        w_words = w_sb[:].bitcast(F32).rearrange("p (a w) -> p a w", a=3)
+        w_grouped = const.tile([P, PASSES * 3 * E * PACK], BF16, align_bytes=64)
+        w_grouped_words = w_grouped[:].bitcast(F32).rearrange("p (g a n u) -> p g a n u", g=PASSES, a=3, u=2)
+        for a in range(3):
+            regroup(w_grouped_words[:, :, a, :, :], transpose_rows(w_words[:, a, :]))
+        w_codes = const.tile([P, PASSES * 3 * E], U32, align_bytes=64)
+        w_scales = const.tile([P, PASSES * 3 * E], U8, align_bytes=64)
+        QK_COLS = (0, 2 * E)
+        V_COLS = (2 * E, 3 * E)
+
+        def w_cols(g, cols):
+            return slice(g * 3 * E + cols[0], g * 3 * E + cols[1])
+
+        for g in range(PASSES):
+            for cols in (QK_COLS, V_COLS):
+                nc.vector.quantize_mx(
+                    out=w_codes[:, w_cols(g, cols)].bitcast(FP8X4),
+                    scales=w_scales[:, w_cols(g, cols)],
+                    in_=w_grouped[:, (g * 3 * E + cols[0]) * PACK : (g * 3 * E + cols[1]) * PACK],
+                )
+
+        def transpose_round(x_sb):
+            x_words = x_sb[:].bitcast(F32).rearrange("p (t w) -> p t w", t=ROUND_TILES)
+            banks = [transpose_rows(x_words[:, t, :]) for t in range(ROUND_TILES)]
+            grouped_pairs = []
+            for pair in range(ROUND_TILES // 2):
+                grouped = grouped_pool.tile([P, 2 * PASSES * P * PACK], BF16, align_bytes=64)
+                grouped_words = grouped[:].bitcast(F32).rearrange("p (t g r u) -> p t g r u", t=2, g=PASSES, u=2)
+                for i in range(2):
+                    regroup(grouped_words[:, i], banks[2 * pair + i])
+                grouped_pairs.append(grouped)
+            return grouped_pairs
+
+        def quantise_round(grouped_pairs):
+            x_codes = code_pool.tile([P, ROUND_TILES * PASSES * P], U32, align_bytes=64)
+            x_scales = code_pool.tile([P, ROUND_TILES * PASSES * P], U8, align_bytes=64)
+            for pair in range(ROUND_TILES // 2):
+                cols = slice(pair * 2 * PASSES * P, (pair + 1) * 2 * PASSES * P)
+                nc.vector.quantize_mx(
+                    out=x_codes[:, cols].bitcast(FP8X4), scales=x_scales[:, cols], in_=grouped_pairs[pair][:]
+                )
+            return x_codes, x_scales
+
+        def multiply(x_codes, x_scales):
+            v_ps = v_pool.tile([P, ROUND_TILES, E], F32)
+            qk_banks = []
+            for pair in range(ROUND_TILES // 2):
+                qk_ps = qk_pool.tile([P, 2, 2 * E], F32)
+                qk_banks.append(qk_ps)
+                for i in range(2):
+                    t = 2 * pair + i
+                    for g in range(PASSES):
+                        tokens = slice((t * PASSES + g) * P, (t * PASSES + g + 1) * P)
+                        for acc, cols in ((qk_ps[:, i, :], QK_COLS), (v_ps[:, t, :], V_COLS)):
+                            nc.tensor.matmul_mx(
+                                out=acc,
+                                lhsT=x_codes[:, tokens].bitcast(FP8X4),
+                                lhsT_scale=x_scales[:, tokens],
+                                rhs=w_codes[:, w_cols(g, cols)].bitcast(FP8X4),
+                                rhs_scale=w_scales[:, w_cols(g, cols)],
+                                start=(g == 0),
+                                stop=(g == PASSES - 1),
+                            )
+            return qk_banks, v_ps
+
+        def rotate(first_pos, qk_banks, v_ps, res_view, slot):
+            sin_part = sin_pool.tile([P, 2 * NH, ROUND_TILES, HD], F32)
+            for pair in range(ROUND_TILES // 2):
+                x = qk_banks[pair][:].rearrange("p t (c d) -> p t c d", d=HD)
+                js = slice(first_pos + 2 * pair, first_pos + 2 * pair + 2)
+                ts = slice(2 * pair, 2 * pair + 2)
+                nc.vector.tensor_tensor(
+                    out=res_view[:, 0 : 2 * NH, slot + 2 * pair : slot + 2 * pair + 2, :].rearrange("p c t d -> p t c d"),
+                    in0=x,
+                    in1=cos_sb[:, js, :].unsqueeze(2).to_broadcast([P, 2, 2 * NH, HD]),
+                    op=MULT,
+                )
+                for dst, src in ((slice(0, HALF), slice(HALF, HD)), (slice(HALF, HD), slice(0, HALF))):
+                    nc.vector.tensor_tensor(
+                        out=sin_part[:, :, ts, dst].rearrange("p c t d -> p t c d"),
+                        in0=x[:, :, :, src],
+                        in1=sin_sb[:, js, dst].unsqueeze(2).to_broadcast([P, 2, 2 * NH, HALF]),
+                        op=MULT,
+                    )
+            rotated = res_view[:, 0 : 2 * NH, slot : slot + ROUND_TILES, :]
+            nc.gpsimd.tensor_tensor(out=rotated, in0=rotated, in1=sin_part[:], op=ADD)
+            nc.scalar.copy(
+                out=res_view[:, 2 * NH : 3 * NH, slot : slot + ROUND_TILES, :],
+                in_=v_ps[:].rearrange("p t (h d) -> p h t d", d=HD),
+            )
+
+        def store(b, first_pos, res_view):
+            for which in range(3):
+                rows = outs[which][b].rearrange("h (p j) d -> p h j d", j=POS)
+                nc.sync.dma_start(
+                    out=rows[:, :, first_pos : first_pos + STORE_TILES, :],
+                    in_=res_view[:, which * NH : (which + 1) * NH, :, :],
+                )
+
+        grouped_rounds = {0: transpose_round(x_tiles[0]), 1: transpose_round(x_tiles[1])}
+        quantised = {0: quantise_round(grouped_rounds[0])}
+        res_view = None
+        for r in range(ROUNDS):
+            b, quarter = divmod(r, ROUNDS_PER_BATCH)
+            first_pos = quarter * ROUND_TILES
+            slot = first_pos % STORE_TILES
+            if r + LOOKAHEAD < ROUNDS:
+                x_tiles[r + LOOKAHEAD] = load_round(r + LOOKAHEAD)
+            if r + 2 < ROUNDS:
+                grouped_rounds[r + 2] = transpose_round(x_tiles[r + 2])
+            if r + 1 < ROUNDS:
+                quantised[r + 1] = quantise_round(grouped_rounds[r + 1])
+            qk_banks, v_ps = multiply(quantised[r][0], quantised[r][1])
+            if slot == 0:
+                res = res_pool.tile([P, 3 * NH, STORE_TILES, HD], F32)
+                res_view = res[:]
+            rotate(first_pos, qk_banks, v_ps, res_view, slot)
+            if slot + ROUND_TILES == STORE_TILES:
+                store(b, first_pos + ROUND_TILES - STORE_TILES, res_view)

@@ -20,11 +20,11 @@ PASSES = H // (P * PACK)
 ROW_WORDS = H // 2
 WORD_BLOCKS = ROW_WORDS // P
 POS = S // P
-ROUND_TILES = 4
+ROUND_TILES = 2
 ROUNDS_PER_BATCH = POS // ROUND_TILES
 ROUNDS = B * ROUNDS_PER_BATCH
 STORE_TILES = 8
-LOOKAHEAD = 5
+LOOKAHEAD = 10
 
 FLOPS = 2 * B * S * H * 3 * E
 

@@ -24,7 +24,8 @@ ROUND_TILES = 2
 ROUNDS_PER_BATCH = POS // ROUND_TILES
 ROUNDS = B * ROUNDS_PER_BATCH
 STORE_TILES = 8
-LOOKAHEAD = 10
+WARM_COLS = 512
+LOOKAHEAD = 20
 
 FLOPS = 2 * B * S * H * 3 * E
 
@@ -46,7 +47,7 @@ def tile_flashattention_pa_t_kernel(tc, hidden_states, cos, sin, w_qkv, out_0, o
         v_pool = ctx.enter_context(tc.psum_pool(name="v", bufs=2))
 
         def transpose_rows(words):
-            xt = xt_pool.tile([P, WORD_BLOCKS, P], F32)
+            xt = xt_pool.tile([P, WORD_BLOCKS, P], F32, name="xt")
             for blk in range(WORD_BLOCKS):
                 g, u = divmod(blk, 2)
                 nc.tensor.transpose(xt[:, blk, :], words[:, 2 * P * g + u : 2 * P * (g + 1) : 2], ident[:])
@@ -58,10 +59,17 @@ def tile_flashattention_pa_t_kernel(tc, hidden_states, cos, sin, w_qkv, out_0, o
         ident = const.tile([P, P], F32)
         make_identity(nc, ident[:])
 
-        w_sb = const.tile([P, 3 * H], BF16)
-        nc.sync.dma_start(
-            out=w_sb[:].rearrange("p (a k) -> p a k", a=3), in_=w_qkv.rearrange("(a p) k -> p a k", p=P)
-        )
+        zeros = const.tile([P, WARM_COLS], BF16)
+        nc.vector.memset(zeros[:], 0.0)
+
+        def warm_up(count):
+            xt = xt_pool.tile([P, WARM_COLS], F32, name="xt")
+            for _ in range(count):
+                nc.tensor.matmul(xt[:], lhsT=zeros[:, 0:P], rhs=zeros[:], start=True, stop=True)
+
+        w_sb = const.tile([P, 3, H], BF16)
+        for a in range(3):
+            nc.sync.dma_start(out=w_sb[:, a, :], in_=w_qkv[a * P : (a + 1) * P, :])
 
         def load_round(r):
             b, quarter = divmod(r, ROUNDS_PER_BATCH)
@@ -70,23 +78,19 @@ def tile_flashattention_pa_t_kernel(tc, hidden_states, cos, sin, w_qkv, out_0, o
             nc.sync.dma_start(out=x_sb[:], in_=rows[:, quarter * ROUND_TILES * H : (quarter + 1) * ROUND_TILES * H])
             return x_sb
 
-        x_tiles = {}
-        x_tiles[0] = load_round(0)
+        x_tiles = {r: load_round(r) for r in range(3)}
 
         cos_sb = const.tile([P, POS, HD], BF16)
         sin_sb = const.tile([P, POS, HD], BF16)
         nc.sync.dma_start(out=cos_sb[:], in_=cos.rearrange("(p j) d -> p j d", j=POS))
         nc.sync.dma_start(out=sin_sb[:], in_=sin.rearrange("(p j) d -> p j d", j=POS))
-        nc.vector.tensor_scalar_mul(out=sin_sb[:, :, 0:HALF], in0=sin_sb[:, :, 0:HALF], scalar1=-1.0)
 
-        for r in range(1, LOOKAHEAD):
+        for r in range(3, LOOKAHEAD):
             x_tiles[r] = load_round(r)
 
-        w_words = w_sb[:].bitcast(F32).rearrange("p (a w) -> p a w", a=3)
+        w_words = w_sb[:].rearrange("p a k -> p (a k)").bitcast(F32).rearrange("p (a w) -> p a w", a=3)
         w_grouped = const.tile([P, PASSES * 3 * E * PACK], BF16, align_bytes=64)
         w_grouped_words = w_grouped[:].bitcast(F32).rearrange("p (g a n u) -> p g a n u", g=PASSES, a=3, u=2)
-        for a in range(3):
-            regroup(w_grouped_words[:, :, a, :, :], transpose_rows(w_words[:, a, :]))
         w_codes = const.tile([P, PASSES * 3 * E], U32, align_bytes=64)
         w_scales = const.tile([P, PASSES * 3 * E], U8, align_bytes=64)
         QK_COLS = (0, 2 * E)
@@ -95,13 +99,17 @@ def tile_flashattention_pa_t_kernel(tc, hidden_states, cos, sin, w_qkv, out_0, o
         def w_cols(g, cols):
             return slice(g * 3 * E + cols[0], g * 3 * E + cols[1])
 
-        for g in range(PASSES):
-            for cols in (QK_COLS, V_COLS):
+        warm_up(6)
+        for a in range(3):
+            regroup(w_grouped_words[:, :, a, :, :], transpose_rows(w_words[:, a, :]))
+            for g in range(PASSES):
+                n = w_cols(g, (a * E, (a + 1) * E))
                 nc.vector.quantize_mx(
-                    out=w_codes[:, w_cols(g, cols)].bitcast(FP8X4),
-                    scales=w_scales[:, w_cols(g, cols)],
-                    in_=w_grouped[:, (g * 3 * E + cols[0]) * PACK : (g * 3 * E + cols[1]) * PACK],
+                    out=w_codes[:, n].bitcast(FP8X4),
+                    scales=w_scales[:, n],
+                    in_=w_grouped[:, n.start * PACK : n.stop * PACK],
                 )
+        warm_up(2)
 
         def transpose_round(x_sb):
             x_words = x_sb[:].bitcast(F32).rearrange("p (t w) -> p t w", t=ROUND_TILES)
@@ -182,6 +190,7 @@ def tile_flashattention_pa_t_kernel(tc, hidden_states, cos, sin, w_qkv, out_0, o
                 )
 
         grouped_rounds = {0: transpose_round(x_tiles[0]), 1: transpose_round(x_tiles[1])}
+        warm_up(2)
         quantised = {0: quantise_round(grouped_rounds[0])}
         res_view = None
         for r in range(ROUNDS):
@@ -194,6 +203,8 @@ def tile_flashattention_pa_t_kernel(tc, hidden_states, cos, sin, w_qkv, out_0, o
                 grouped_rounds[r + 2] = transpose_round(x_tiles[r + 2])
             if r + 1 < ROUNDS:
                 quantised[r + 1] = quantise_round(grouped_rounds[r + 1])
+            if r == 0:
+                nc.vector.tensor_scalar_mul(out=sin_sb[:, :, 0:HALF], in0=sin_sb[:, :, 0:HALF], scalar1=-1.0)
             qk_banks, v_ps = multiply(quantised[r][0], quantised[r][1])
             if slot == 0:
                 res = res_pool.tile([P, 3 * NH, STORE_TILES, HD], F32)

@@ -25,7 +25,7 @@ ROUNDS_PER_BATCH = POS // ROUND_TILES
 ROUNDS = B * ROUNDS_PER_BATCH
 STORE_TILES = 8
 WARM_COLS = 512
-LOOKAHEAD = 20
+LOOKAHEAD = 11
 
 FLOPS = 2 * B * S * H * 3 * E
 
@@ -41,7 +41,7 @@ def tile_flashattention_pa_t_kernel(tc, hidden_states, cos, sin, w_qkv, out_0, o
         grouped_pool = ctx.enter_context(tc.tile_pool(name="grouped", bufs=6))
         code_pool = ctx.enter_context(tc.tile_pool(name="codes", bufs=3))
         sin_pool = ctx.enter_context(tc.tile_pool(name="sin_part", bufs=3))
-        res_pool = ctx.enter_context(tc.tile_pool(name="res", bufs=3))
+        res_pool = ctx.enter_context(tc.tile_pool(name="res", bufs=4))
         xt_pool = ctx.enter_context(tc.psum_pool(name="xt", bufs=4))
         qk_pool = ctx.enter_context(tc.psum_pool(name="qk", bufs=2))
         v_pool = ctx.enter_context(tc.psum_pool(name="v", bufs=2))

@@ -157,42 +157,54 @@ def tile_flashattention_pa_t_kernel(tc, hidden_states, cos, sin, w_qkv, out_0, o
 
         def rotate(first_pos, qk_banks, v_ps, res_view, slot):
             sin_part = sin_pool.tile([P, 2 * NH, ROUND_TILES, HD], F32)
-            for pair in range(ROUND_TILES // 2):
-                x = qk_banks[pair][:].rearrange("p t (c d) -> p t c d", d=HD)
-                js = slice(first_pos + 2 * pair, first_pos + 2 * pair + 2)
-                ts = slice(2 * pair, 2 * pair + 2)
-                nc.vector.tensor_tensor(
-                    out=res_view[:, 0 : 2 * NH, slot + 2 * pair : slot + 2 * pair + 2, :].rearrange("p c t d -> p t c d"),
-                    in0=x,
-                    in1=cos_sb[:, js, :].unsqueeze(2).to_broadcast([P, 2, 2 * NH, HD]),
-                    op=MULT,
-                )
-                for dst, src in ((slice(0, HALF), slice(HALF, HD)), (slice(HALF, HD), slice(0, HALF))):
-                    nc.vector.tensor_tensor(
-                        out=sin_part[:, :, ts, dst].rearrange("p c t d -> p t c d"),
-                        in0=x[:, :, :, src],
-                        in1=sin_sb[:, js, dst].unsqueeze(2).to_broadcast([P, 2, 2 * NH, HALF]),
-                        op=MULT,
-                    )
+            js = slice(first_pos, first_pos + ROUND_TILES)
+            shape = [P, ROUND_TILES, 2 * NH, HD]
             rotated = res_view[:, 0 : 2 * NH, slot : slot + ROUND_TILES, :]
-            nc.gpsimd.tensor_tensor(out=rotated, in0=rotated, in1=sin_part[:], op=ADD)
+            x = qk_banks[0][:].rearrange("p t (c d) -> p t c d", d=HD)
+            nc.vector.tensor_tensor(
+                out=rotated.rearrange("p c t d -> p t c d"),
+                in0=x,
+                in1=cos_sb[:, js, :].unsqueeze(2).to_broadcast(shape),
+                op=MULT,
+            )
+            in_halves = [P, ROUND_TILES, 2 * NH, 2, HALF]
+            nc.vector.tensor_tensor(
+                out=sin_part[:].rearrange("p c t (h d) -> p t c h d", h=2),
+                in0=x.rearrange("p t c (h d) -> p t c h d", h=2)[:, :, :, ::-1, :],
+                in1=sin_sb[:, js, :].rearrange("p t (h d) -> p t h d", h=2).unsqueeze(2).to_broadcast(in_halves),
+                op=MULT,
+            )
             nc.scalar.copy(
                 out=res_view[:, 2 * NH : 3 * NH, slot : slot + ROUND_TILES, :],
                 in_=v_ps[:].rearrange("p t (h d) -> p h t d", d=HD),
             )
+            return rotated, sin_part
 
-        def store(b, first_pos, res_view):
-            for which in range(3):
+        def add(engine, parts, rotated, sin_part):
+            engine.tensor_tensor(out=rotated[:, parts], in0=rotated[:, parts], in1=sin_part[:, parts], op=ADD)
+
+        def store(b, first_pos, slot, count, res_view):
+            for which in (2, 0, 1):
                 rows = outs[which][b].rearrange("h (p j) d -> p h j d", j=POS)
                 nc.sync.dma_start(
-                    out=rows[:, :, first_pos : first_pos + STORE_TILES, :],
-                    in_=res_view[:, which * NH : (which + 1) * NH, :, :],
+                    out=rows[:, :, first_pos : first_pos + count, :],
+                    in_=res_view[:, which * NH : (which + 1) * NH, slot : slot + count, :],
                 )
 
         grouped_rounds = {0: transpose_round(x_tiles[0]), 1: transpose_round(x_tiles[1])}
         warm_up(2)
         quantised = {0: quantise_round(grouped_rounds[0])}
+        G_PARTS, V_PARTS = slice(0, 3), slice(3, 4)
+        pending = None
+
+        def finish(store_args, rotated, sin_part):
+            add(nc.vector, V_PARTS, rotated, sin_part)
+            add(nc.gpsimd, G_PARTS, rotated, sin_part)
+            if store_args is not None:
+                store(*store_args)
+
         res_view = None
+        stored = 0
         for r in range(ROUNDS):
             b, quarter = divmod(r, ROUNDS_PER_BATCH)
             first_pos = quarter * ROUND_TILES
@@ -203,12 +215,20 @@ def tile_flashattention_pa_t_kernel(tc, hidden_states, cos, sin, w_qkv, out_0, o
                 grouped_rounds[r + 2] = transpose_round(x_tiles[r + 2])
             if r + 1 < ROUNDS:
                 quantised[r + 1] = quantise_round(grouped_rounds[r + 1])
+            if pending is not None:
+                finish(*pending)
             if r == 0:
                 nc.vector.tensor_scalar_mul(out=sin_sb[:, :, 0:HALF], in0=sin_sb[:, :, 0:HALF], scalar1=-1.0)
             qk_banks, v_ps = multiply(quantised[r][0], quantised[r][1])
             if slot == 0:
                 res = res_pool.tile([P, 3 * NH, STORE_TILES, HD], F32)
                 res_view = res[:]
-            rotate(first_pos, qk_banks, v_ps, res_view, slot)
-            if slot + ROUND_TILES == STORE_TILES:
-                store(b, first_pos + ROUND_TILES - STORE_TILES, res_view)
+            rotated, sin_part = rotate(first_pos, qk_banks, v_ps, res_view, slot)
+            stored += ROUND_TILES
+            store_args = None
+            if slot + ROUND_TILES == STORE_TILES or r >= ROUNDS - 3:
+                store_args = (b, first_pos + ROUND_TILES - stored, slot + ROUND_TILES - stored, stored, res_view)
+                stored = 0
+            pending = (store_args, rotated, sin_part)
+        add(nc.vector, slice(0, 2 * NH), rotated, sin_part)
+        store(*store_args)

@@ -23,9 +23,11 @@ POS = S // P
 ROUND_TILES = 2
 ROUNDS_PER_BATCH = POS // ROUND_TILES
 ROUNDS = B * ROUNDS_PER_BATCH
-STORE_TILES = 8
+STORE_TILES = POS
+LAST_STORES = (8, 12, 14, 16)
 WARM_COLS = 512
-LOOKAHEAD = 11
+LOAD_ROUNDS = 4
+LOOKAHEAD = 12
 
 FLOPS = 2 * B * S * H * 3 * E
 
@@ -37,11 +39,11 @@ def tile_flashattention_pa_t_kernel(tc, hidden_states, cos, sin, w_qkv, out_0, o
     with ExitStack() as ctx:
         ctx.enter_context(tc.manual_schedule())
         const = ctx.enter_context(tc.tile_pool(name="const", bufs=1))
-        x_pool = ctx.enter_context(tc.tile_pool(name="x", bufs=LOOKAHEAD))
-        grouped_pool = ctx.enter_context(tc.tile_pool(name="grouped", bufs=6))
+        x_pool = ctx.enter_context(tc.tile_pool(name="x", bufs=4))
+        grouped_pool = ctx.enter_context(tc.tile_pool(name="grouped", bufs=4))
         code_pool = ctx.enter_context(tc.tile_pool(name="codes", bufs=3))
         sin_pool = ctx.enter_context(tc.tile_pool(name="sin_part", bufs=3))
-        res_pool = ctx.enter_context(tc.tile_pool(name="res", bufs=4))
+        res_pool = ctx.enter_context(tc.tile_pool(name="res", bufs=3))
         xt_pool = ctx.enter_context(tc.psum_pool(name="xt", bufs=4))
         qk_pool = ctx.enter_context(tc.psum_pool(name="qk", bufs=2))
         v_pool = ctx.enter_context(tc.psum_pool(name="v", bufs=2))
@@ -71,22 +73,37 @@ def tile_flashattention_pa_t_kernel(tc, hidden_states, cos, sin, w_qkv, out_0, o
         for a in range(3):
             nc.sync.dma_start(out=w_sb[:, a, :], in_=w_qkv[a * P : (a + 1) * P, :])
 
-        def load_round(r):
-            b, quarter = divmod(r, ROUNDS_PER_BATCH)
-            x_sb = x_pool.tile([P, ROUND_TILES * H], BF16)
-            rows = hidden_states[b].rearrange("(p j) k -> p (j k)", j=POS)
-            nc.sync.dma_start(out=x_sb[:], in_=rows[:, quarter * ROUND_TILES * H : (quarter + 1) * ROUND_TILES * H])
-            return x_sb
+        x_words = {}
 
-        x_tiles = {r: load_round(r) for r in range(3)}
+        def load_rounds(x_sb, first, count):
+            b, quarter = divmod(first, ROUNDS_PER_BATCH)
+            rows = hidden_states[b].rearrange("(p j) k -> p (j k)", j=POS)
+            nc.sync.dma_start(out=x_sb, in_=rows[:, quarter * ROUND_TILES * H : (quarter + count) * ROUND_TILES * H])
+            words = x_sb.bitcast(F32).rearrange("p (r t w) -> p r t w", r=count, t=ROUND_TILES)
+            for i in range(count):
+                x_words[first + i] = words[:, i, :, :]
+
+        x_first = const.tile([P, ROUNDS_PER_BATCH * ROUND_TILES * H], BF16)
+
+        def load_first(first, count):
+            load_rounds(x_first[:, first * ROUND_TILES * H : (first + count) * ROUND_TILES * H], first, count)
+
+        def load_next(first):
+            x_sb = x_pool.tile([P, LOAD_ROUNDS * ROUND_TILES * H], BF16)
+            load_rounds(x_sb[:], first, LOAD_ROUNDS)
+
+        load_first(0, 1)
+        load_first(1, 1)
+        load_first(2, 2)
 
         cos_sb = const.tile([P, POS, HD], BF16)
         sin_sb = const.tile([P, POS, HD], BF16)
         nc.sync.dma_start(out=cos_sb[:], in_=cos.rearrange("(p j) d -> p j d", j=POS))
         nc.sync.dma_start(out=sin_sb[:], in_=sin.rearrange("(p j) d -> p j d", j=POS))
 
-        for r in range(3, LOOKAHEAD):
-            x_tiles[r] = load_round(r)
+        load_first(4, 2)
+        load_first(6, 2)
+        load_next(8)
 
         w_words = w_sb[:].rearrange("p a k -> p (a k)").bitcast(F32).rearrange("p (a w) -> p a w", a=3)
         w_grouped = const.tile([P, PASSES * 3 * E * PACK], BF16, align_bytes=64)
@@ -111,9 +128,8 @@ def tile_flashattention_pa_t_kernel(tc, hidden_states, cos, sin, w_qkv, out_0, o
                 )
         warm_up(2)
 
-        def transpose_round(x_sb):
-            x_words = x_sb[:].bitcast(F32).rearrange("p (t w) -> p t w", t=ROUND_TILES)
-            banks = [transpose_rows(x_words[:, t, :]) for t in range(ROUND_TILES)]
+        def transpose_round(words):
+            banks = [transpose_rows(words[:, t, :]) for t in range(ROUND_TILES)]
             grouped_pairs = []
             for pair in range(ROUND_TILES // 2):
                 grouped = grouped_pool.tile([P, 2 * PASSES * P * PACK], BF16, align_bytes=64)
@@ -139,13 +155,12 @@ def tile_flashattention_pa_t_kernel(tc, hidden_states, cos, sin, w_qkv, out_0, o
             for pair in range(ROUND_TILES // 2):
                 qk_ps = qk_pool.tile([P, 2, 2 * E], F32)
                 qk_banks.append(qk_ps)
-                for i in range(2):
-                    t = 2 * pair + i
-                    for g in range(PASSES):
-                        tokens = slice((t * PASSES + g) * P, (t * PASSES + g + 1) * P)
-                        for acc, cols in ((qk_ps[:, i, :], QK_COLS), (v_ps[:, t, :], V_COLS)):
+                for banks, cols in ((qk_ps, QK_COLS), (v_ps, V_COLS)):
+                    for t in range(2):
+                        for g in range(PASSES):
+                            tokens = slice((t * PASSES + g) * P, (t * PASSES + g + 1) * P)
                             nc.tensor.matmul_mx(
-                                out=acc,
+                                out=banks[:, t, :],
                                 lhsT=x_codes[:, tokens].bitcast(FP8X4),
                                 lhsT_scale=x_scales[:, tokens],
                                 rhs=w_codes[:, w_cols(g, cols)].bitcast(FP8X4),
@@ -155,53 +170,58 @@ def tile_flashattention_pa_t_kernel(tc, hidden_states, cos, sin, w_qkv, out_0, o
                             )
             return qk_banks, v_ps
 
-        def rotate(first_pos, qk_banks, v_ps, res_view, slot):
-            sin_part = sin_pool.tile([P, 2 * NH, ROUND_TILES, HD], F32)
-            js = slice(first_pos, first_pos + ROUND_TILES)
-            shape = [P, ROUND_TILES, 2 * NH, HD]
-            rotated = res_view[:, 0 : 2 * NH, slot : slot + ROUND_TILES, :]
-            x = qk_banks[0][:].rearrange("p t (c d) -> p t c d", d=HD)
+        def times_cos(cs, first_pos, qk_ps, rotated):
             nc.vector.tensor_tensor(
-                out=rotated.rearrange("p c t d -> p t c d"),
-                in0=x,
-                in1=cos_sb[:, js, :].unsqueeze(2).to_broadcast(shape),
+                out=rotated[:, cs].rearrange("p c t d -> p t c d"),
+                in0=qk_ps[:].rearrange("p t (c d) -> p t c d", d=HD)[:, :, cs, :],
+                in1=cos_sb[:, first_pos : first_pos + ROUND_TILES, :]
+                .unsqueeze(2)
+                .to_broadcast([P, ROUND_TILES, cs.stop - cs.start, HD]),
                 op=MULT,
             )
-            in_halves = [P, ROUND_TILES, 2 * NH, 2, HALF]
+
+        def times_sin(ts, first_pos, qk_ps, sin_part):
+            count = ts.stop - ts.start
             nc.vector.tensor_tensor(
-                out=sin_part[:].rearrange("p c t (h d) -> p t c h d", h=2),
-                in0=x.rearrange("p t c (h d) -> p t c h d", h=2)[:, :, :, ::-1, :],
-                in1=sin_sb[:, js, :].rearrange("p t (h d) -> p t h d", h=2).unsqueeze(2).to_broadcast(in_halves),
+                out=sin_part[:, :, ts, :].rearrange("p c t (h d) -> p t c h d", h=2),
+                in0=qk_ps[:, ts, :].rearrange("p t (c h d) -> p t c h d", h=2, d=HALF)[:, :, :, ::-1, :],
+                in1=sin_sb[:, first_pos + ts.start : first_pos + ts.stop, :]
+                .rearrange("p t (h d) -> p t h d", h=2)
+                .unsqueeze(2)
+                .to_broadcast([P, count, 2 * NH, 2, HALF]),
                 op=MULT,
             )
+
+        def copy_v(v_ps, res_view, slot):
             nc.scalar.copy(
                 out=res_view[:, 2 * NH : 3 * NH, slot : slot + ROUND_TILES, :],
                 in_=v_ps[:].rearrange("p t (h d) -> p h t d", d=HD),
             )
-            return rotated, sin_part
 
         def add(engine, parts, rotated, sin_part):
             engine.tensor_tensor(out=rotated[:, parts], in0=rotated[:, parts], in1=sin_part[:, parts], op=ADD)
 
-        def store(b, first_pos, slot, count, res_view):
-            for which in (2, 0, 1):
-                rows = outs[which][b].rearrange("h (p j) d -> p h j d", j=POS)
-                nc.sync.dma_start(
-                    out=rows[:, :, first_pos : first_pos + count, :],
-                    in_=res_view[:, which * NH : (which + 1) * NH, slot : slot + count, :],
-                )
+        def store(which, b, first_pos, slot, count, res_view):
+            rows = outs[which][b].rearrange("h (p j) d -> p h j d", j=POS)
+            nc.sync.dma_start(
+                out=rows[:, :, first_pos : first_pos + count, :],
+                in_=res_view[:, which * NH : (which + 1) * NH, slot : slot + count, :],
+            )
 
-        grouped_rounds = {0: transpose_round(x_tiles[0]), 1: transpose_round(x_tiles[1])}
+        grouped_rounds = {0: transpose_round(x_words[0]), 1: transpose_round(x_words[1])}
         warm_up(2)
         quantised = {0: quantise_round(grouped_rounds[0])}
-        G_PARTS, V_PARTS = slice(0, 3), slice(3, 4)
+        Q_PART, K_PART, BOTH = slice(0, NH), slice(NH, 2 * NH), slice(0, 2 * NH)
+        G_PART, V_PART = slice(0, 3), slice(3, 4)
         pending = None
 
-        def finish(store_args, rotated, sin_part):
-            add(nc.vector, V_PARTS, rotated, sin_part)
-            add(nc.gpsimd, G_PARTS, rotated, sin_part)
+        def finish(store_args, rotated, sin_part, shared):
+            if shared:
+                add(nc.vector, V_PART, rotated, sin_part)
+            add(nc.gpsimd, G_PART if shared else BOTH, rotated, sin_part)
             if store_args is not None:
-                store(*store_args)
+                for which in (2, 0, 1):
+                    store(which, *store_args)
 
         res_view = None
         stored = 0
@@ -209,26 +229,38 @@ def tile_flashattention_pa_t_kernel(tc, hidden_states, cos, sin, w_qkv, out_0, o
             b, quarter = divmod(r, ROUNDS_PER_BATCH)
             first_pos = quarter * ROUND_TILES
             slot = first_pos % STORE_TILES
-            if r + LOOKAHEAD < ROUNDS:
-                x_tiles[r + LOOKAHEAD] = load_round(r + LOOKAHEAD)
+            if r % LOAD_ROUNDS == 0 and r + LOOKAHEAD < ROUNDS:
+                load_next(r + LOOKAHEAD)
             if r + 2 < ROUNDS:
-                grouped_rounds[r + 2] = transpose_round(x_tiles[r + 2])
+                grouped_rounds[r + 2] = transpose_round(x_words[r + 2])
             if r + 1 < ROUNDS:
                 quantised[r + 1] = quantise_round(grouped_rounds[r + 1])
             if pending is not None:
-                finish(*pending)
+                finish(*pending, shared=r < ROUNDS - 2)
             if r == 0:
                 nc.vector.tensor_scalar_mul(out=sin_sb[:, :, 0:HALF], in0=sin_sb[:, :, 0:HALF], scalar1=-1.0)
             qk_banks, v_ps = multiply(quantised[r][0], quantised[r][1])
             if slot == 0:
                 res = res_pool.tile([P, 3 * NH, STORE_TILES, HD], F32)
                 res_view = res[:]
-            rotated, sin_part = rotate(first_pos, qk_banks, v_ps, res_view, slot)
+            rotated = res_view[:, BOTH, slot : slot + ROUND_TILES, :]
+            sin_part = sin_pool.tile([P, 2 * NH, ROUND_TILES, HD], F32)
+            if r < ROUNDS - 1:
+                times_cos(BOTH, first_pos, qk_banks[0], rotated)
+                times_sin(slice(0, ROUND_TILES), first_pos, qk_banks[0], sin_part)
+            else:
+                times_cos(Q_PART, first_pos, qk_banks[0], rotated)
+                for t in range(ROUND_TILES):
+                    times_sin(slice(t, t + 1), first_pos, qk_banks[0], sin_part)
+                times_cos(K_PART, first_pos, qk_banks[0], rotated)
+            copy_v(v_ps, res_view, slot)
             stored += ROUND_TILES
             store_args = None
-            if slot + ROUND_TILES == STORE_TILES or r >= ROUNDS - 3:
+            if slot + ROUND_TILES in (LAST_STORES if b == B - 1 else (STORE_TILES,)):
                 store_args = (b, first_pos + ROUND_TILES - stored, slot + ROUND_TILES - stored, stored, res_view)
                 stored = 0
             pending = (store_args, rotated, sin_part)
-        add(nc.vector, slice(0, 2 * NH), rotated, sin_part)
-        store(*store_args)
+        store(2, *store_args)
+        for which, part in ((0, Q_PART), (1, K_PART)):
+            add(nc.vector, part, rotated, sin_part)
+            store(which, *store_args)

@@ -26,6 +26,7 @@ ROUNDS = B * ROUNDS_PER_BATCH
 STORE_TILES = POS
 LAST_STORES = (8, 12, 14, 16)
 WARM_COLS = 512
+SORT_EVERY, SORT_FROM = 3, 3
 LOAD_ROUNDS = 4
 LOOKAHEAD = 12
 
@@ -41,6 +42,7 @@ def tile_flashattention_pa_t_kernel(tc, hidden_states, cos, sin, w_qkv, out_0, o
         const = ctx.enter_context(tc.tile_pool(name="const", bufs=1))
         x_pool = ctx.enter_context(tc.tile_pool(name="x", bufs=4))
         grouped_pool = ctx.enter_context(tc.tile_pool(name="grouped", bufs=4))
+        sort_pool = ctx.enter_context(tc.tile_pool(name="sorted", bufs=3))
         code_pool = ctx.enter_context(tc.tile_pool(name="codes", bufs=3))
         sin_pool = ctx.enter_context(tc.tile_pool(name="sin_part", bufs=3))
         res_pool = ctx.enter_context(tc.tile_pool(name="res", bufs=3))
@@ -53,6 +55,20 @@ def tile_flashattention_pa_t_kernel(tc, hidden_states, cos, sin, w_qkv, out_0, o
             for blk in range(WORD_BLOCKS):
                 g, u = divmod(blk, 2)
                 nc.tensor.transpose(xt[:, blk, :], words[:, 2 * P * g + u : 2 * P * (g + 1) : 2], ident[:])
+            return xt
+
+        def sort_words(words):
+            in_order = sort_pool.tile([P, ROW_WORDS], F32)
+            nc.scalar.copy(
+                out=in_order[:].rearrange("p (g u m) -> p g u m", g=PASSES, u=2),
+                in_=words.rearrange("p (g m u) -> p g u m", g=PASSES, u=2),
+            )
+            return in_order
+
+        def transpose_sorted_rows(in_order):
+            xt = xt_pool.tile([P, WORD_BLOCKS, P], F32, name="xt")
+            for blk in range(WORD_BLOCKS):
+                nc.tensor.transpose(xt[:, blk, :], in_order[:, blk * P : (blk + 1) * P], ident[:])
             return xt
 
         def regroup(dst_words, xt):
@@ -128,8 +144,11 @@ def tile_flashattention_pa_t_kernel(tc, hidden_states, cos, sin, w_qkv, out_0, o
                 )
         warm_up(2)
 
-        def transpose_round(words):
-            banks = [transpose_rows(words[:, t, :]) for t in range(ROUND_TILES)]
+        def transpose_round(r):
+            words = x_words[r]
+            banks = [transpose_rows(words[:, t, :]) for t in range(ROUND_TILES - 1)]
+            last = ROUND_TILES - 1
+            banks.append(transpose_sorted_rows(sorted_words[r]) if r in sorted_words else transpose_rows(words[:, last, :]))
             grouped_pairs = []
             for pair in range(ROUND_TILES // 2):
                 grouped = grouped_pool.tile([P, 2 * PASSES * P * PACK], BF16, align_bytes=64)
@@ -208,7 +227,8 @@ def tile_flashattention_pa_t_kernel(tc, hidden_states, cos, sin, w_qkv, out_0, o
                 in_=res_view[:, which * NH : (which + 1) * NH, slot : slot + count, :],
             )
 
-        grouped_rounds = {0: transpose_round(x_words[0]), 1: transpose_round(x_words[1])}
+        sorted_words = {}
+        grouped_rounds = {0: transpose_round(0), 1: transpose_round(1)}
         warm_up(2)
         quantised = {0: quantise_round(grouped_rounds[0])}
         Q_PART, K_PART, BOTH = slice(0, NH), slice(NH, 2 * NH), slice(0, 2 * NH)
@@ -232,7 +252,9 @@ def tile_flashattention_pa_t_kernel(tc, hidden_states, cos, sin, w_qkv, out_0, o
             if r % LOAD_ROUNDS == 0 and r + LOOKAHEAD < ROUNDS:
                 load_next(r + LOOKAHEAD)
             if r + 2 < ROUNDS:
-                grouped_rounds[r + 2] = transpose_round(x_words[r + 2])
+                grouped_rounds[r + 2] = transpose_round(r + 2)
+            if r + 4 < ROUNDS and r >= SORT_FROM and r % SORT_EVERY == 0:
+                sorted_words[r + 4] = sort_words(x_words[r + 4][:, ROUND_TILES - 1, :])
             if r + 1 < ROUNDS:
                 quantised[r + 1] = quantise_round(grouped_rounds[r + 1])
             if pending is not None:

from contextlib import ExitStack

import concourse.mybir as mybir
from concourse.masks import make_identity

BF16 = mybir.dt.bfloat16
F32 = mybir.dt.float32
U32 = mybir.dt.uint32
U8 = mybir.dt.uint8
FP8X4 = mybir.dt.float8_e4m3fn_x4
MULT = mybir.AluOpType.mult
ADD = mybir.AluOpType.add

B, S, H, NH, HD = 4, 2048, 1024, 2, 64
E = NH * HD
HALF = HD // 2
P = 128
PACK = 4
PASSES = H // (P * PACK)
ROW_WORDS = H // 2
WORD_BLOCKS = ROW_WORDS // P
POS = S // P
ROUND_TILES = 2
ROUNDS_PER_BATCH = POS // ROUND_TILES
ROUNDS = B * ROUNDS_PER_BATCH
STORE_TILES = POS
LAST_STORES = (8, 12, 14, 16)
WARM_COLS = 512
SORT_EVERY, SORT_FROM = 3, 3
LOAD_ROUNDS = 4
LOOKAHEAD = 12

FLOPS = 2 * B * S * H * 3 * E


def tile_flashattention_pa_t_kernel(tc, hidden_states, cos, sin, w_qkv, out_0, out_1, out_2):
    nc = tc.nc
    outs = (out_0, out_1, out_2)

    with ExitStack() as ctx:
        ctx.enter_context(tc.manual_schedule())
        const = ctx.enter_context(tc.tile_pool(name="const", bufs=1))
        x_pool = ctx.enter_context(tc.tile_pool(name="x", bufs=4))
        grouped_pool = ctx.enter_context(tc.tile_pool(name="grouped", bufs=4))
        sort_pool = ctx.enter_context(tc.tile_pool(name="sorted", bufs=3))
        code_pool = ctx.enter_context(tc.tile_pool(name="codes", bufs=3))
        sin_pool = ctx.enter_context(tc.tile_pool(name="sin_part", bufs=3))
        res_pool = ctx.enter_context(tc.tile_pool(name="res", bufs=3))
        xt_pool = ctx.enter_context(tc.psum_pool(name="xt", bufs=4))
        qk_pool = ctx.enter_context(tc.psum_pool(name="qk", bufs=2))
        v_pool = ctx.enter_context(tc.psum_pool(name="v", bufs=2))

        def transpose_rows(words):
            xt = xt_pool.tile([P, WORD_BLOCKS, P], F32, name="xt")
            for blk in range(WORD_BLOCKS):
                g, u = divmod(blk, 2)
                nc.tensor.transpose(xt[:, blk, :], words[:, 2 * P * g + u : 2 * P * (g + 1) : 2], ident[:])
            return xt

        def sort_words(words):
            in_order = sort_pool.tile([P, ROW_WORDS], F32)
            nc.scalar.copy(
                out=in_order[:].rearrange("p (g u m) -> p g u m", g=PASSES, u=2),
                in_=words.rearrange("p (g m u) -> p g u m", g=PASSES, u=2),
            )
            return in_order

        def transpose_sorted_rows(in_order):
            xt = xt_pool.tile([P, WORD_BLOCKS, P], F32, name="xt")
            for blk in range(WORD_BLOCKS):
                nc.tensor.transpose(xt[:, blk, :], in_order[:, blk * P : (blk + 1) * P], ident[:])
            return xt

        def regroup(dst_words, xt):
            nc.scalar.copy(out=dst_words, in_=xt[:].rearrange("p (g u) r -> p g r u", u=2))

        ident = const.tile([P, P], F32)
        make_identity(nc, ident[:])

        zeros = const.tile([P, WARM_COLS], BF16)
        nc.vector.memset(zeros[:], 0.0)

        def warm_up(count):
            xt = xt_pool.tile([P, WARM_COLS], F32, name="xt")
            for _ in range(count):
                nc.tensor.matmul(xt[:], lhsT=zeros[:, 0:P], rhs=zeros[:], start=True, stop=True)

        w_sb = const.tile([P, 3, H], BF16)
        for a in range(3):
            nc.sync.dma_start(out=w_sb[:, a, :], in_=w_qkv[a * P : (a + 1) * P, :])

        x_words = {}

        def load_rounds(x_sb, first, count):
            b, quarter = divmod(first, ROUNDS_PER_BATCH)
            rows = hidden_states[b].rearrange("(p j) k -> p (j k)", j=POS)
            nc.sync.dma_start(out=x_sb, in_=rows[:, quarter * ROUND_TILES * H : (quarter + count) * ROUND_TILES * H])
            words = x_sb.bitcast(F32).rearrange("p (r t w) -> p r t w", r=count, t=ROUND_TILES)
            for i in range(count):
                x_words[first + i] = words[:, i, :, :]

        x_first = const.tile([P, ROUNDS_PER_BATCH * ROUND_TILES * H], BF16)

        def load_first(first, count):
            load_rounds(x_first[:, first * ROUND_TILES * H : (first + count) * ROUND_TILES * H], first, count)

        def load_next(first):
            x_sb = x_pool.tile([P, LOAD_ROUNDS * ROUND_TILES * H], BF16)
            load_rounds(x_sb[:], first, LOAD_ROUNDS)

        load_first(0, 1)
        load_first(1, 1)
        load_first(2, 2)

        cos_sb = const.tile([P, POS, HD], BF16)
        sin_sb = const.tile([P, POS, HD], BF16)
        nc.sync.dma_start(out=cos_sb[:], in_=cos.rearrange("(p j) d -> p j d", j=POS))
        nc.sync.dma_start(out=sin_sb[:], in_=sin.rearrange("(p j) d -> p j d", j=POS))

        load_first(4, 2)
        load_first(6, 2)
        load_next(8)

        w_words = w_sb[:].rearrange("p a k -> p (a k)").bitcast(F32).rearrange("p (a w) -> p a w", a=3)
        w_grouped = const.tile([P, PASSES * 3 * E * PACK], BF16, align_bytes=64)
        w_grouped_words = w_grouped[:].bitcast(F32).rearrange("p (g a n u) -> p g a n u", g=PASSES, a=3, u=2)
        w_codes = const.tile([P, PASSES * 3 * E], U32, align_bytes=64)
        w_scales = const.tile([P, PASSES * 3 * E], U8, align_bytes=64)
        QK_COLS = (0, 2 * E)
        V_COLS = (2 * E, 3 * E)

        def w_cols(g, cols):
            return slice(g * 3 * E + cols[0], g * 3 * E + cols[1])

        warm_up(6)
        for a in range(3):
            regroup(w_grouped_words[:, :, a, :, :], transpose_rows(w_words[:, a, :]))
            for g in range(PASSES):
                n = w_cols(g, (a * E, (a + 1) * E))
                nc.vector.quantize_mx(
                    out=w_codes[:, n].bitcast(FP8X4),
                    scales=w_scales[:, n],
                    in_=w_grouped[:, n.start * PACK : n.stop * PACK],
                )
        warm_up(2)

        def transpose_round(r):
            words = x_words[r]
            banks = [transpose_rows(words[:, t, :]) for t in range(ROUND_TILES - 1)]
            last = ROUND_TILES - 1
            banks.append(transpose_sorted_rows(sorted_words[r]) if r in sorted_words else transpose_rows(words[:, last, :]))
            grouped_pairs = []
            for pair in range(ROUND_TILES // 2):
                grouped = grouped_pool.tile([P, 2 * PASSES * P * PACK], BF16, align_bytes=64)
                grouped_words = grouped[:].bitcast(F32).rearrange("p (t g r u) -> p t g r u", t=2, g=PASSES, u=2)
                for i in range(2):
                    regroup(grouped_words[:, i], banks[2 * pair + i])
                grouped_pairs.append(grouped)
            return grouped_pairs

        def quantise_round(grouped_pairs):
            x_codes = code_pool.tile([P, ROUND_TILES * PASSES * P], U32, align_bytes=64)
            x_scales = code_pool.tile([P, ROUND_TILES * PASSES * P], U8, align_bytes=64)
            for pair in range(ROUND_TILES // 2):
                cols = slice(pair * 2 * PASSES * P, (pair + 1) * 2 * PASSES * P)
                nc.vector.quantize_mx(
                    out=x_codes[:, cols].bitcast(FP8X4), scales=x_scales[:, cols], in_=grouped_pairs[pair][:]
                )
            return x_codes, x_scales

        def multiply(x_codes, x_scales):
            v_ps = v_pool.tile([P, ROUND_TILES, E], F32)
            qk_banks = []
            for pair in range(ROUND_TILES // 2):
                qk_ps = qk_pool.tile([P, 2, 2 * E], F32)
                qk_banks.append(qk_ps)
                for banks, cols in ((qk_ps, QK_COLS), (v_ps, V_COLS)):
                    for t in range(2):
                        for g in range(PASSES):
                            tokens = slice((t * PASSES + g) * P, (t * PASSES + g + 1) * P)
                            nc.tensor.matmul_mx(
                                out=banks[:, t, :],
                                lhsT=x_codes[:, tokens].bitcast(FP8X4),
                                lhsT_scale=x_scales[:, tokens],
                                rhs=w_codes[:, w_cols(g, cols)].bitcast(FP8X4),
                                rhs_scale=w_scales[:, w_cols(g, cols)],
                                start=(g == 0),
                                stop=(g == PASSES - 1),
                            )
            return qk_banks, v_ps

        def times_cos(cs, first_pos, qk_ps, rotated):
            nc.vector.tensor_tensor(
                out=rotated[:, cs].rearrange("p c t d -> p t c d"),
                in0=qk_ps[:].rearrange("p t (c d) -> p t c d", d=HD)[:, :, cs, :],
                in1=cos_sb[:, first_pos : first_pos + ROUND_TILES, :]
                .unsqueeze(2)
                .to_broadcast([P, ROUND_TILES, cs.stop - cs.start, HD]),
                op=MULT,
            )

        def times_sin(ts, first_pos, qk_ps, sin_part):
            count = ts.stop - ts.start
            nc.vector.tensor_tensor(
                out=sin_part[:, :, ts, :].rearrange("p c t (h d) -> p t c h d", h=2),
                in0=qk_ps[:, ts, :].rearrange("p t (c h d) -> p t c h d", h=2, d=HALF)[:, :, :, ::-1, :],
                in1=sin_sb[:, first_pos + ts.start : first_pos + ts.stop, :]
                .rearrange("p t (h d) -> p t h d", h=2)
                .unsqueeze(2)
                .to_broadcast([P, count, 2 * NH, 2, HALF]),
                op=MULT,
            )

        def copy_v(v_ps, res_view, slot):
            nc.scalar.copy(
                out=res_view[:, 2 * NH : 3 * NH, slot : slot + ROUND_TILES, :],
                in_=v_ps[:].rearrange("p t (h d) -> p h t d", d=HD),
            )

        def add(engine, parts, rotated, sin_part):
            engine.tensor_tensor(out=rotated[:, parts], in0=rotated[:, parts], in1=sin_part[:, parts], op=ADD)

        def store(which, b, first_pos, slot, count, res_view):
            rows = outs[which][b].rearrange("h (p j) d -> p h j d", j=POS)
            nc.sync.dma_start(
                out=rows[:, :, first_pos : first_pos + count, :],
                in_=res_view[:, which * NH : (which + 1) * NH, slot : slot + count, :],
            )

        sorted_words = {}
        grouped_rounds = {0: transpose_round(0), 1: transpose_round(1)}
        warm_up(2)
        quantised = {0: quantise_round(grouped_rounds[0])}
        Q_PART, K_PART, BOTH = slice(0, NH), slice(NH, 2 * NH), slice(0, 2 * NH)
        G_PART, V_PART = slice(0, 3), slice(3, 4)
        pending = None

        def finish(store_args, rotated, sin_part, shared):
            if shared:
                add(nc.vector, V_PART, rotated, sin_part)
            add(nc.gpsimd, G_PART if shared else BOTH, rotated, sin_part)
            if store_args is not None:
                for which in (2, 0, 1):
                    store(which, *store_args)

        res_view = None
        stored = 0
        for r in range(ROUNDS):
            b, quarter = divmod(r, ROUNDS_PER_BATCH)
            first_pos = quarter * ROUND_TILES
            slot = first_pos % STORE_TILES
            if r % LOAD_ROUNDS == 0 and r + LOOKAHEAD < ROUNDS:
                load_next(r + LOOKAHEAD)
            if r + 2 < ROUNDS:
                grouped_rounds[r + 2] = transpose_round(r + 2)
            if r + 4 < ROUNDS and r >= SORT_FROM and r % SORT_EVERY == 0:
                sorted_words[r + 4] = sort_words(x_words[r + 4][:, ROUND_TILES - 1, :])
            if r + 1 < ROUNDS:
                quantised[r + 1] = quantise_round(grouped_rounds[r + 1])
            if pending is not None:
                finish(*pending, shared=r < ROUNDS - 2)
            if r == 0:
                nc.vector.tensor_scalar_mul(out=sin_sb[:, :, 0:HALF], in0=sin_sb[:, :, 0:HALF], scalar1=-1.0)
            qk_banks, v_ps = multiply(quantised[r][0], quantised[r][1])
            if slot == 0:
                res = res_pool.tile([P, 3 * NH, STORE_TILES, HD], F32)
                res_view = res[:]
            rotated = res_view[:, BOTH, slot : slot + ROUND_TILES, :]
            sin_part = sin_pool.tile([P, 2 * NH, ROUND_TILES, HD], F32)
            if r < ROUNDS - 1:
                times_cos(BOTH, first_pos, qk_banks[0], rotated)
                times_sin(slice(0, ROUND_TILES), first_pos, qk_banks[0], sin_part)
            else:
                times_cos(Q_PART, first_pos, qk_banks[0], rotated)
                for t in range(ROUND_TILES):
                    times_sin(slice(t, t + 1), first_pos, qk_banks[0], sin_part)
                times_cos(K_PART, first_pos, qk_banks[0], rotated)
            copy_v(v_ps, res_view, slot)
            stored += ROUND_TILES
            store_args = None
            if slot + ROUND_TILES in (LAST_STORES if b == B - 1 else (STORE_TILES,)):
                store_args = (b, first_pos + ROUND_TILES - stored, slot + ROUND_TILES - stored, stored, res_view)
                stored = 0
            pending = (store_args, rotated, sin_part)
        store(2, *store_args)
        for which, part in ((0, Q_PART), (1, K_PART)):
            add(nc.vector, part, rotated, sin_part)
            store(which, *store_args)
